import numpy as np
import ml_dtypes


def mxq(x, axis, fmt="e4m3"):
    dtype, down = {"e4m3": (ml_dtypes.float8_e4m3fn, 7), "e5m2": (ml_dtypes.float8_e5m2, 14)}[fmt]
    v = np.moveaxis(np.asarray(x, np.float32).astype(ml_dtypes.bfloat16).astype(np.float64), axis, -1)
    blocks = v.reshape(v.shape[:-1] + (-1, 32))
    amax = np.abs(blocks).max(-1, keepdims=True)
    byte = np.maximum(np.where(amax > 0, np.frexp(amax)[1] - 1 + 127, 0) - down, 1)
    scale = np.exp2(byte - 127.0)
    codes = (blocks / scale).astype(np.float32).astype(dtype).astype(np.float64)
    return np.moveaxis((codes * scale).reshape(v.shape), -1, axis)


WIDE = False


def mx_kscale(k):
    if not WIDE:
        return np.ones(k)
    levels = np.array([10, -10, 5, -5, 0])
    a = np.random.permutation(np.resize(levels, k // 512 * 4)).reshape(k // 512, 4)
    idx = np.arange(k)
    return np.exp2(a[idx // 512, idx % 128 // 32])


BF16 = ml_dtypes.bfloat16


def bf(x):
    return np.asarray(x, np.float32).astype(BF16)


def f64(x):
    return np.asarray(x).astype(np.float64)


E2M1 = np.array([0.0, 0.5, 1.0, 1.5, 2.0, 3.0, 4.0, 6.0, -0.0, -0.5, -1.0, -1.5, -2.0, -3.0, -4.0, -6.0])


def pack_weight(w, fmt):
    k, n = w.shape
    w = f64(bf(w)).reshape(k // 32, 32, n)
    amax = np.abs(w).max(1)
    if fmt == "e4m3":
        byte = np.frexp(amax)[1] - 1 + 127 - 7
    else:
        mant, ex = np.frexp(amax / 6.0)
        byte = np.where(mant > 0.5, ex, ex - 1) + 127
    byte = np.clip(np.where(amax > 0, byte, 1), 1, 254)
    scaled = (w * np.exp2(127.0 - byte)[:, None, :]).reshape(k, n).astype(np.float32)
    by_word = np.ascontiguousarray(scaled.reshape(k // 512, 128, 4, n).transpose(0, 1, 3, 2))
    if fmt == "e4m3":
        words = by_word.astype(ml_dtypes.float8_e4m3fn).view(np.uint8)
    else:
        c = by_word.astype(ml_dtypes.float4_e2m1fn).view(np.uint8) & 0xF
        words = c[..., 0::2] | (c[..., 1::2] << 4)
    return np.ascontiguousarray(words), np.ascontiguousarray(byte.astype(np.uint8).reshape(k // 512, 16, n))


def unpack_weight(words, scales, fmt):
    g, p, n, _ = words.shape
    if fmt == "e4m3":
        vals = np.ascontiguousarray(words).view(ml_dtypes.float8_e4m3fn).astype(np.float64)
    else:
        nib = np.empty((g, p, n, 4), np.uint8)
        nib[..., 0::2] = words & 0xF
        nib[..., 1::2] = words >> 4
        vals = E2M1[nib]
    vals = vals * np.repeat(np.exp2(scales.astype(np.float64) - 127.0), 8, axis=1)[..., None]
    return vals.transpose(0, 1, 3, 2).reshape(g * 512, n)


T, BLK, B, NH, NW, C, K = 16, 4, 4, 4, 4, 1024, 512
R = B * NH * NW
HAD = np.array([[1.0, 1.0, 1.0, 1.0],
                [1.0, -1.0, 1.0, -1.0],
                [1.0, 1.0, -1.0, -1.0],
                [1.0, -1.0, -1.0, 1.0]])


def setup_inputs():
    s = mx_kscale(C)
    trans = bf(np.random.standard_normal((T, B, NH, NW, C)) * s)
    stack = np.random.standard_normal((T, C, K)) * 2.0 / np.sqrt(C) / s[None, :, None]
    words, scales = pack_weight(stack.reshape(-1, K), "e4m3")
    bias = bf(np.random.standard_normal((1, 1, 1, K)) * 0.2)
    return {"trans": trans,
            "weight_words": words,
            "weight_scales": scales,
            "bias": bias}


def reference(trans, weight_words, weight_scales, bias):
    mixed = mxq(f64(trans).reshape(T, R, C), 2, "e4m3") @ unpack_weight(weight_words, weight_scales, "e4m3").reshape(T, C, K)
    mixed = mixed.reshape(BLK, BLK, B, NH, NW, K)
    out = np.zeros((B, NH, BLK, NW, BLK, K))
    for i in range(BLK):
        for j in range(BLK):
            acc = np.zeros((B, NH, NW, K))
            for u in range(BLK):
                for v in range(BLK):
                    acc = acc + HAD[i, u] * HAD[j, v] * mixed[u, v]
            out[:, :, i, :, j, :] = acc
    out = out * (1.0 / T)
    return out.reshape(B, NH * BLK, NW * BLK, K) + f64(bias)

@@ -1,0 +1,210 @@
+from contextlib import ExitStack
+
+import concourse.mybir as mybir
+from concourse.masks import make_identity
+
+F32 = mybir.dt.float32
+BF16 = mybir.dt.bfloat16
+I32 = mybir.dt.int32
+U32 = mybir.dt.uint32
+U8 = mybir.dt.uint8
+FP8X4 = mybir.dt.float8_e4m3fn_x4
+MULT = mybir.AluOpType.mult
+ADD = mybir.AluOpType.add
+
+P = 128
+COEFFS = 16
+ROWS = 64
+CHANNELS = 1024
+N_OUT = 512
+PACK = 4
+K_PASS = P * PACK
+PASSES = CHANNELS // K_PASS
+PHASES = 4
+H4 = ((1, 1, 1, 1), (1, -1, 1, -1), (1, 1, -1, -1), (1, -1, -1, 1))
+
+FLOPS = 2 * COEFFS * ROWS * CHANNELS * N_OUT
+
+
+def tile_iwht2layer_pa_e_kernel(tc, trans, weight_words, weight_scales, bias, out):
+    nc = tc.nc
+    with ExitStack() as ctx:
+        const = ctx.enter_context(tc.tile_pool(name="const", bufs=1))
+        resident = ctx.enter_context(tc.tile_pool(name="resident", bufs=1))
+        stage = ctx.enter_context(tc.tile_pool(name="stage", bufs=4))
+        operands = ctx.enter_context(tc.tile_pool(name="operands", bufs=8))
+        sums = ctx.enter_context(tc.tile_pool(name="sums", bufs=22))
+        psum_x = ctx.enter_context(tc.psum_pool(name="psum_x", bufs=4))
+        psum_z = ctx.enter_context(tc.psum_pool(name="psum_z", bufs=4))
+
+        x_view = trans.rearrange("t b h w c -> (t b h w) c").rearrange(
+            "(hi q p) c -> q p hi c", hi=2, q=PHASES, p=P
+        )
+        w_view = weight_words.rearrange("g p n t -> p g (n t)")
+        s_view = weight_scales.rearrange("(a k) (quad r) n -> k r quad a n", k=4, r=4)
+        out_view = out.rearrange(
+            "b (h i1 i0) (w j1 j0) n -> i0 j1 j0 (b h i1) w n", i1=2, i0=2, j1=2, j0=2
+        )
+
+        w_planes = const.tile([P, COEFFS // 2, N_OUT], U8, align_bytes=64)
+        nc.vector.memset(w_planes[:].bitcast(I32), 0)
+        for k in range(4):
+            for r in range(4):
+                nc.sync.dma_start(
+                    out=w_planes[4 * k + r : P : 32, :, :].bitcast(I32),
+                    in_=s_view[k, r].bitcast(I32),
+                )
+
+        bias_row = const.tile([P, N_OUT], BF16)
+        nc.vector.memset(bias_row[:], 0.0)
+        nc.scalar.dma_start(out=bias_row[0:1, :], in_=bias.rearrange("a b c n -> (a b c) n"))
+
+        x_sb = []
+        w_sb = {}
+
+        def load_x(q):
+            x_tile = resident.tile([P, 2, CHANNELS], BF16, name="x%d" % q)
+            nc.sync.dma_start(out=x_tile[:], in_=x_view[q])
+            x_sb.append(x_tile)
+
+        def load_w(q):
+            for hi in range(2):
+                for lo in range(2):
+                    t = 2 * (4 * hi + q) + lo
+                    w_tile = resident.tile([P, PASSES, N_OUT], U32, name="w%d" % t, align_bytes=64)
+                    nc.sync.dma_start(
+                        out=w_tile[:].bitcast(I32),
+                        in_=w_view[:, PASSES * t : PASSES * (t + 1), :].bitcast(I32),
+                    )
+                    w_sb[t] = w_tile
+
+        load_x(0)
+        load_x(1)
+        load_w(0)
+        load_x(2)
+        load_w(1)
+        load_x(3)
+        load_w(2)
+        load_w(3)
+
+        ident = const.tile([P, P], F32)
+        make_identity(nc, ident[:])
+        ones = const.tile([P, P], BF16)
+        nc.vector.memset(ones[:], 1.0)
+
+        codes_of = {}
+        scales_of = {}
+
+        def prepare(q):
+            for hi in range(2):
+                x_words = x_sb[q][:, hi, :].bitcast(F32)
+                x_t = psum_x.tile([P, PASSES, 2, P], F32)
+                for g in range(PASSES):
+                    for half in range(2):
+                        first = (K_PASS // 2) * g + half
+                        nc.tensor.transpose(
+                            x_t[:, g, half, :],
+                            x_words[:, first : (K_PASS // 2) * (g + 1) : 2],
+                            ident[:],
+                        )
+                grouped_of = []
+                for lo in range(2):
+                    variants = 1 + lo
+                    grouped = stage.tile(
+                        [P, variants * PASSES * K_PASS], BF16, align_bytes=64, name="grouped%d" % lo
+                    )
+                    grouped_of.append(grouped)
+                    as_words = grouped[:].bitcast(F32).rearrange(
+                        "p (s g m i w e) -> p s g m i w e", s=variants, g=PASSES, m=16, i=2, w=4, e=2
+                    )
+                    source = x_t[:, :, :, ROWS * lo : ROWS * (lo + 1)].rearrange(
+                        "p g e (m w) -> p g m w e", w=4
+                    )
+                    nc.scalar.copy(out=as_words[:, 0, :, :, 0, :, :], in_=source)
+                    if hi == 0:
+                        nc.scalar.copy(out=as_words[:, 0, :, :, 1, :, :], in_=source)
+                if hi == 1:
+                    for lo in range(2):
+                        halves = grouped_of[lo][:, 0 : PASSES * K_PASS].rearrange(
+                            "p (m i c) -> p m i c", i=2, c=16
+                        )
+                        nc.scalar.mul(out=halves[:, :, 1, :], in_=halves[:, :, 0, :], mul=-1.0)
+                nc.scalar.mul(
+                    out=grouped_of[1][:, PASSES * K_PASS :],
+                    in_=grouped_of[1][:, 0 : PASSES * K_PASS],
+                    mul=-1.0,
+                )
+                for lo in range(2):
+                    variants = 1 + lo
+                    t = 2 * (4 * hi + q) + lo
+                    codes = operands.tile(
+                        [P, variants * PASSES * P], U32, align_bytes=64, name="codes%d" % lo
+                    )
+                    x_scales = operands.tile(
+                        [P, variants * PASSES * P], U8, align_bytes=64, name="x_scales%d" % lo
+                    )
+                    nc.vector.quantize_mx(
+                        out=codes[:].bitcast(FP8X4), scales=x_scales[:], in_=grouped_of[lo][:]
+                    )
+                    codes_of[t] = codes
+                    scales_of[t] = x_scales
+
+        def multiply(q):
+            z_of = []
+            for j0 in range(2):
+                z = psum_z.tile([P, N_OUT], F32, name="z")
+                z_of.append(z)
+            for hi in range(2):
+                for lo in range(2):
+                    t = 2 * (4 * hi + q) + lo
+                    for j0 in range(2):
+                        for g in range(PASSES):
+                            cols = slice((j0 * lo * PASSES + g) * P, (j0 * lo * PASSES + g + 1) * P)
+                            plane = 4 * (PASSES * lo + g)
+                            nc.tensor.matmul_mx(
+                                out=z_of[j0][:],
+                                lhsT=codes_of[t][:, cols].bitcast(FP8X4),
+                                lhsT_scale=scales_of[t][:, cols],
+                                rhs=w_sb[t][:, g, :].bitcast(FP8X4),
+                                rhs_scale=w_planes[plane:P, 4 * hi + q, :],
+                                start=(hi == 0 and lo == 0 and g == 0),
+                                stop=(hi == 1 and lo == 1 and g == PASSES - 1),
+                            )
+            return z_of
+
+        partial = [{}, {}]
+
+        def combine(q, z_of):
+            for j0 in range(2):
+                fresh = {}
+                for o in range(4):
+                    signs = H4[o][: q + 1]
+                    if signs in fresh:
+                        continue
+                    earlier = partial[j0][signs[:-1]] if q > 0 else bias_all
+                    acc = sums.tile([P, N_OUT], F32, name="acc")
+                    nc.vector.scalar_tensor_tensor(
+                        out=acc[:],
+                        in0=z_of[j0][:],
+                        scalar=signs[-1] / 16.0,
+                        in1=earlier[:],
+                        op0=MULT,
+                        op1=ADD,
+                    )
+                    fresh[signs] = acc
+                    if q == PHASES - 1:
+                        i0, j1 = divmod(o, 2)
+                        nc.sync.dma_start(out=out_view[i0, j1, j0], in_=acc[:])
+                partial[j0] = fresh
+
+        prepare(0)
+
+        bias_ps = psum_z.tile([P, N_OUT], F32, name="z")
+        nc.tensor.matmul(out=bias_ps[:], lhsT=ones[:], rhs=bias_row[:], start=True, stop=True)
+        bias_all = const.tile([P, N_OUT], F32)
+        nc.scalar.copy(out=bias_all[:], in_=bias_ps[:])
+
+        for q in range(PHASES):
+            if q + 1 < PHASES:
+                prepare(q + 1)
+            combine(q, multiply(q))

@@ -129,10 +129,10 @@ def tile_iwht2layer_pa_e_kernel(tc, trans, weight_words, weight_scales, bias, ou
                             "p (m i c) -> p m i c", i=2, c=16
                         )
                         nc.scalar.mul(out=halves[:, :, 1, :], in_=halves[:, :, 0, :], mul=-1.0)
-                nc.scalar.mul(
+                nc.vector.tensor_scalar_mul(
                     out=grouped_of[1][:, PASSES * K_PASS :],
-                    in_=grouped_of[1][:, 0 : PASSES * K_PASS],
-                    mul=-1.0,
+                    in0=grouped_of[1][:, 0 : PASSES * K_PASS],
+                    scalar1=-1.0,
                 )
                 for lo in range(2):
                     variants = 1 + lo

@@ -41,19 +41,21 @@ def tile_iwht2layer_pa_e_kernel(tc, trans, weight_words, weight_scales, bias, ou
             "(hi q p) c -> q p hi c", hi=2, q=PHASES, p=P
         )
         w_view = weight_words.rearrange("g p n t -> p g (n t)")
-        s_view = weight_scales.rearrange("(a k) (quad r) n -> k r quad a n", k=4, r=4)
+        s_view = weight_scales.rearrange("(a k) (quad r) n -> quad r k a n", k=4, r=4)
         out_view = out.rearrange(
             "b (h i1 i0) (w j1 j0) n -> i0 j1 j0 (b h i1) w n", i1=2, i0=2, j1=2, j0=2
         )
 
         w_planes = const.tile([P, COEFFS // 2, N_OUT], U8, align_bytes=64)
         nc.vector.memset(w_planes[:].bitcast(I32), 0)
-        for k in range(4):
-            for r in range(4):
-                nc.sync.dma_start(
-                    out=w_planes[4 * k + r : P : 32, :, :].bitcast(I32),
-                    in_=s_view[k, r].bitcast(I32),
-                )
+
+        def load_scales():
+            for quad in range(4):
+                for r in range(4):
+                    nc.sync.dma_start(
+                        out=w_planes[32 * quad + r : 32 * quad + 16 : 4, :, :].bitcast(I32),
+                        in_=s_view[quad, r].bitcast(I32),
+                    )
 
         bias_row = const.tile([P, N_OUT], BF16)
         nc.vector.memset(bias_row[:], 0.0)
@@ -79,6 +81,7 @@ def tile_iwht2layer_pa_e_kernel(tc, trans, weight_words, weight_scales, bias, ou
                     w_sb[t] = w_tile
 
         load_x(0)
+        load_scales()
         load_x(1)
         load_w(0)
         load_x(2)
@@ -198,6 +201,7 @@ def tile_iwht2layer_pa_e_kernel(tc, trans, weight_words, weight_scales, bias, ou
                 partial[j0] = fresh
 
         prepare(0)
+        prepare(1)
 
         bias_ps = psum_z.tile([P, N_OUT], F32, name="z")
         nc.tensor.matmul(out=bias_ps[:], lhsT=ones[:], rhs=bias_row[:], start=True, stop=True)
@@ -205,6 +209,6 @@ def tile_iwht2layer_pa_e_kernel(tc, trans, weight_words, weight_scales, bias, ou
         nc.scalar.copy(out=bias_all[:], in_=bias_ps[:])
 
         for q in range(PHASES):
-            if q + 1 < PHASES:
-                prepare(q + 1)
             combine(q, multiply(q))
+            if q + 2 < PHASES:
+                prepare(q + 2)

@@ -36,6 +36,7 @@ def tile_iwht2layer_pa_e_kernel(tc, trans, weight_words, weight_scales, bias, ou
         sums = ctx.enter_context(tc.tile_pool(name="sums", bufs=22))
         psum_x = ctx.enter_context(tc.psum_pool(name="psum_x", bufs=4))
         psum_z = ctx.enter_context(tc.psum_pool(name="psum_z", bufs=4))
+        ctx.enter_context(tc.manual_schedule())
 
         x_view = trans.rearrange("t b h w c -> (t b h w) c").rearrange(
             "(hi q p) c -> q p hi c", hi=2, q=PHASES, p=P

@@ -14,16 +14,34 @@ ADD = mybir.AluOpType.add
 
 P = 128
 COEFFS = 16
-ROWS = 64
+BLOCKS = 64
+BH = 16
+W = 4
 CHANNELS = 1024
 N_OUT = 512
 PACK = 4
 K_PASS = P * PACK
 PASSES = CHANNELS // K_PASS
+PASS_WORDS = K_PASS // 2
 PHASES = 4
+PAIRS = COEFFS // 2
+PLANES = 2 * PASSES
+QUADS = 4
+QUAD_P = P // QUADS
+QUAD_ROWS = 4
+AHEAD = 2
 H4 = ((1, 1, 1, 1), (1, -1, 1, -1), (1, 1, -1, -1), (1, -1, -1, 1))
+SUMS = 2 * (1 + 2 + 4 + 4)
 
-FLOPS = 2 * COEFFS * ROWS * CHANNELS * N_OUT
+FLOPS = 2 * COEFFS * BLOCKS * CHANNELS * N_OUT
+
+
+def pair_index(phase, u1):
+    return PHASES * u1 + phase
+
+
+def coefficient(phase, u1, v0):
+    return 2 * pair_index(phase, u1) + v0
 
 
 def tile_iwht2layer_pa_e_kernel(tc, trans, weight_words, weight_scales, bias, out):
@@ -31,185 +49,187 @@ def tile_iwht2layer_pa_e_kernel(tc, trans, weight_words, weight_scales, bias, ou
     with ExitStack() as ctx:
         const = ctx.enter_context(tc.tile_pool(name="const", bufs=1))
         resident = ctx.enter_context(tc.tile_pool(name="resident", bufs=1))
-        stage = ctx.enter_context(tc.tile_pool(name="stage", bufs=4))
-        operands = ctx.enter_context(tc.tile_pool(name="operands", bufs=8))
-        sums = ctx.enter_context(tc.tile_pool(name="sums", bufs=22))
-        psum_x = ctx.enter_context(tc.psum_pool(name="psum_x", bufs=4))
-        psum_z = ctx.enter_context(tc.psum_pool(name="psum_z", bufs=4))
-        ctx.enter_context(tc.manual_schedule())
+        stage = ctx.enter_context(tc.tile_pool(name="stage", bufs=2 * AHEAD))
+        operands = ctx.enter_context(tc.tile_pool(name="operands", bufs=2 * (AHEAD + 1)))
+        sums = ctx.enter_context(tc.tile_pool(name="sums", bufs=SUMS))
+        psum_x = ctx.enter_context(tc.psum_pool(name="psum_x", bufs=2 * AHEAD))
+        psum_z = ctx.enter_context(tc.psum_pool(name="psum_z", bufs=2 * 2))
 
         x_view = trans.rearrange("t b h w c -> (t b h w) c").rearrange(
-            "(hi q p) c -> q p hi c", hi=2, q=PHASES, p=P
+            "(u1 phase p) c -> phase p u1 c", u1=2, phase=PHASES, p=P
         )
-        w_view = weight_words.rearrange("g p n t -> p g (n t)")
-        s_view = weight_scales.rearrange("(a k) (quad r) n -> quad r k a n", k=4, r=4)
+        w_view = weight_words.rearrange("g p n e -> p g (n e)")
+        s_view = weight_scales.rearrange(
+            "(pair plane) (quad r) n -> quad r plane pair n", plane=PLANES, r=QUAD_ROWS
+        )
         out_view = out.rearrange(
             "b (h i1 i0) (w j1 j0) n -> i0 j1 j0 (b h i1) w n", i1=2, i0=2, j1=2, j0=2
         )
 
-        w_planes = const.tile([P, COEFFS // 2, N_OUT], U8, align_bytes=64)
+        x_of = {}
+        w_of = {}
+
+        def load_x(phase):
+            x_sb = resident.tile([P, 2, CHANNELS], BF16, name="x%d" % phase)
+            nc.sync.dma_start(out=x_sb[:], in_=x_view[phase])
+            x_of[phase] = x_sb
+
+        def load_w(phase):
+            for u1 in range(2):
+                for v0 in range(2):
+                    t = coefficient(phase, u1, v0)
+                    w_sb = resident.tile([P, PASSES, N_OUT], U32, name="w%d" % t, align_bytes=64)
+                    nc.sync.dma_start(
+                        out=w_sb[:].bitcast(I32),
+                        in_=w_view[:, PASSES * t : PASSES * (t + 1), :].bitcast(I32),
+                    )
+                    w_of[t] = w_sb
+
+        w_planes = const.tile([P, PAIRS, N_OUT], U8, align_bytes=64)
         nc.vector.memset(w_planes[:].bitcast(I32), 0)
 
         def load_scales():
-            for quad in range(4):
-                for r in range(4):
+            for quad in range(QUADS):
+                for r in range(QUAD_ROWS):
+                    first = QUAD_P * quad + r
                     nc.sync.dma_start(
-                        out=w_planes[32 * quad + r : 32 * quad + 16 : 4, :, :].bitcast(I32),
+                        out=w_planes[first : first + QUAD_ROWS * PLANES : QUAD_ROWS, :, :].bitcast(I32),
                         in_=s_view[quad, r].bitcast(I32),
                     )
-
-        bias_row = const.tile([P, N_OUT], BF16)
-        nc.vector.memset(bias_row[:], 0.0)
-        nc.scalar.dma_start(out=bias_row[0:1, :], in_=bias.rearrange("a b c n -> (a b c) n"))
-
-        x_sb = []
-        w_sb = {}
-
-        def load_x(q):
-            x_tile = resident.tile([P, 2, CHANNELS], BF16, name="x%d" % q)
-            nc.sync.dma_start(out=x_tile[:], in_=x_view[q])
-            x_sb.append(x_tile)
-
-        def load_w(q):
-            for hi in range(2):
-                for lo in range(2):
-                    t = 2 * (4 * hi + q) + lo
-                    w_tile = resident.tile([P, PASSES, N_OUT], U32, name="w%d" % t, align_bytes=64)
-                    nc.sync.dma_start(
-                        out=w_tile[:].bitcast(I32),
-                        in_=w_view[:, PASSES * t : PASSES * (t + 1), :].bitcast(I32),
-                    )
-                    w_sb[t] = w_tile
 
         load_x(0)
         load_scales()
         load_x(1)
-        load_w(0)
-        load_x(2)
-        load_w(1)
-        load_x(3)
-        load_w(2)
-        load_w(3)
+        for phase in range(PHASES):
+            load_w(phase)
+            if phase + AHEAD < PHASES:
+                load_x(phase + AHEAD)
 
         ident = const.tile([P, P], F32)
         make_identity(nc, ident[:])
         ones = const.tile([P, P], BF16)
         nc.vector.memset(ones[:], 1.0)
+        bias_row = const.tile([P, N_OUT], BF16)
+        nc.vector.memset(bias_row[:], 0.0)
+        nc.scalar.dma_start(out=bias_row[0:1, :], in_=bias.rearrange("a b c n -> (a b c) n"))
+        bias_all = const.tile([P, N_OUT], F32)
+
+        def spread_bias():
+            bias_ps = psum_z.tile([P, N_OUT], F32, name="z")
+            nc.tensor.matmul(out=bias_ps[:], lhsT=ones[:], rhs=bias_row[:], start=True, stop=True)
+            nc.scalar.copy(out=bias_all[:], in_=bias_ps[:])
 
         codes_of = {}
         scales_of = {}
 
-        def prepare(q):
-            for hi in range(2):
-                x_words = x_sb[q][:, hi, :].bitcast(F32)
+        def prepare(phase):
+            for u1 in range(2):
+                x_words = x_of[phase][:, u1, :].bitcast(F32)
                 x_t = psum_x.tile([P, PASSES, 2, P], F32)
                 for g in range(PASSES):
                     for half in range(2):
-                        first = (K_PASS // 2) * g + half
                         nc.tensor.transpose(
                             x_t[:, g, half, :],
-                            x_words[:, first : (K_PASS // 2) * (g + 1) : 2],
+                            x_words[:, PASS_WORDS * g + half : PASS_WORDS * (g + 1) : 2],
                             ident[:],
                         )
+
                 grouped_of = []
-                for lo in range(2):
-                    variants = 1 + lo
+                for v0 in range(2):
+                    copies = 1 + v0
                     grouped = stage.tile(
-                        [P, variants * PASSES * K_PASS], BF16, align_bytes=64, name="grouped%d" % lo
+                        [P, copies * PASSES * K_PASS], BF16, align_bytes=64, name="grouped%d" % v0
                     )
                     grouped_of.append(grouped)
                     as_words = grouped[:].bitcast(F32).rearrange(
-                        "p (s g m i w e) -> p s g m i w e", s=variants, g=PASSES, m=16, i=2, w=4, e=2
+                        "p (copy g m i1 w half) -> p copy g m i1 w half",
+                        copy=copies, g=PASSES, m=BH, i1=2, w=W, half=2,
                     )
-                    source = x_t[:, :, :, ROWS * lo : ROWS * (lo + 1)].rearrange(
-                        "p g e (m w) -> p g m w e", w=4
+                    rows = x_t[:, :, :, BLOCKS * v0 : BLOCKS * (v0 + 1)].rearrange(
+                        "p g half (m w) -> p g m w half", w=W
                     )
-                    nc.scalar.copy(out=as_words[:, 0, :, :, 0, :, :], in_=source)
-                    if hi == 0:
-                        nc.scalar.copy(out=as_words[:, 0, :, :, 1, :, :], in_=source)
-                if hi == 1:
-                    for lo in range(2):
-                        halves = grouped_of[lo][:, 0 : PASSES * K_PASS].rearrange(
-                            "p (m i c) -> p m i c", i=2, c=16
+                    nc.scalar.copy(out=as_words[:, 0, :, :, 0, :, :], in_=rows)
+                    if u1 == 0:
+                        nc.scalar.copy(out=as_words[:, 0, :, :, 1, :, :], in_=rows)
+                if u1 == 1:
+                    for v0 in range(2):
+                        by_i1 = grouped_of[v0][:, 0 : PASSES * K_PASS].rearrange(
+                            "p (gm i1 wc) -> p gm i1 wc", i1=2, wc=W * PACK
                         )
-                        nc.scalar.mul(out=halves[:, :, 1, :], in_=halves[:, :, 0, :], mul=-1.0)
+                        nc.scalar.mul(out=by_i1[:, :, 1, :], in_=by_i1[:, :, 0, :], mul=-1.0)
+
                 nc.vector.tensor_scalar_mul(
                     out=grouped_of[1][:, PASSES * K_PASS :],
                     in0=grouped_of[1][:, 0 : PASSES * K_PASS],
                     scalar1=-1.0,
                 )
-                for lo in range(2):
-                    variants = 1 + lo
-                    t = 2 * (4 * hi + q) + lo
+                for v0 in range(2):
+                    copies = 1 + v0
+                    t = coefficient(phase, u1, v0)
                     codes = operands.tile(
-                        [P, variants * PASSES * P], U32, align_bytes=64, name="codes%d" % lo
+                        [P, copies * PASSES * P], U32, align_bytes=64, name="codes%d" % v0
                     )
                     x_scales = operands.tile(
-                        [P, variants * PASSES * P], U8, align_bytes=64, name="x_scales%d" % lo
+                        [P, copies * PASSES * P], U8, align_bytes=64, name="x_scales%d" % v0
                     )
                     nc.vector.quantize_mx(
-                        out=codes[:].bitcast(FP8X4), scales=x_scales[:], in_=grouped_of[lo][:]
+                        out=codes[:].bitcast(FP8X4), scales=x_scales[:], in_=grouped_of[v0][:]
                     )
                     codes_of[t] = codes
                     scales_of[t] = x_scales
 
-        def multiply(q):
+        def multiply(phase):
             z_of = []
             for j0 in range(2):
                 z = psum_z.tile([P, N_OUT], F32, name="z")
                 z_of.append(z)
-            for hi in range(2):
-                for lo in range(2):
-                    t = 2 * (4 * hi + q) + lo
+            for u1 in range(2):
+                for v0 in range(2):
+                    t = coefficient(phase, u1, v0)
                     for j0 in range(2):
+                        copy = j0 * v0
                         for g in range(PASSES):
-                            cols = slice((j0 * lo * PASSES + g) * P, (j0 * lo * PASSES + g + 1) * P)
-                            plane = 4 * (PASSES * lo + g)
+                            cols = slice((copy * PASSES + g) * P, (copy * PASSES + g + 1) * P)
+                            k = QUAD_ROWS * (PASSES * v0 + g)
                             nc.tensor.matmul_mx(
                                 out=z_of[j0][:],
                                 lhsT=codes_of[t][:, cols].bitcast(FP8X4),
                                 lhsT_scale=scales_of[t][:, cols],
-                                rhs=w_sb[t][:, g, :].bitcast(FP8X4),
-                                rhs_scale=w_planes[plane:P, 4 * hi + q, :],
-                                start=(hi == 0 and lo == 0 and g == 0),
-                                stop=(hi == 1 and lo == 1 and g == PASSES - 1),
+                                rhs=w_of[t][:, g, :].bitcast(FP8X4),
+                                rhs_scale=w_planes[k:P, pair_index(phase, u1), :],
+                                start=(u1 == 0 and v0 == 0 and g == 0),
+                                stop=(u1 == 1 and v0 == 1 and g == PASSES - 1),
                             )
             return z_of
 
-        partial = [{}, {}]
+        sum_of = [{(): bias_all}, {(): bias_all}]
 
-        def combine(q, z_of):
+        def combine(phase, z_of):
             for j0 in range(2):
-                fresh = {}
-                for o in range(4):
-                    signs = H4[o][: q + 1]
-                    if signs in fresh:
+                longer = {}
+                for o in range(len(H4)):
+                    signs = H4[o][: phase + 1]
+                    if signs in longer:
                         continue
-                    earlier = partial[j0][signs[:-1]] if q > 0 else bias_all
                     acc = sums.tile([P, N_OUT], F32, name="acc")
                     nc.vector.scalar_tensor_tensor(
                         out=acc[:],
                         in0=z_of[j0][:],
-                        scalar=signs[-1] / 16.0,
-                        in1=earlier[:],
+                        scalar=signs[-1] / COEFFS,
+                        in1=sum_of[j0][signs[:-1]][:],
                         op0=MULT,
                         op1=ADD,
                     )
-                    fresh[signs] = acc
-                    if q == PHASES - 1:
+                    longer[signs] = acc
+                    if phase == PHASES - 1:
                         i0, j1 = divmod(o, 2)
                         nc.sync.dma_start(out=out_view[i0, j1, j0], in_=acc[:])
-                partial[j0] = fresh
+                sum_of[j0] = longer
 
-        prepare(0)
-        prepare(1)
-
-        bias_ps = psum_z.tile([P, N_OUT], F32, name="z")
-        nc.tensor.matmul(out=bias_ps[:], lhsT=ones[:], rhs=bias_row[:], start=True, stop=True)
-        bias_all = const.tile([P, N_OUT], F32)
-        nc.scalar.copy(out=bias_all[:], in_=bias_ps[:])
-
-        for q in range(PHASES):
-            combine(q, multiply(q))
-            if q + 2 < PHASES:
-                prepare(q + 2)
+        for phase in range(AHEAD):
+            prepare(phase)
+        spread_bias()
+        for phase in range(PHASES):
+            combine(phase, multiply(phase))
+            if phase + AHEAD < PHASES:
+                prepare(phase + AHEAD)

@@ -11,6 +11,7 @@ U8 = mybir.dt.uint8
 FP8X4 = mybir.dt.float8_e4m3fn_x4
 MULT = mybir.AluOpType.mult
 ADD = mybir.AluOpType.add
+SUBTRACT = mybir.AluOpType.subtract
 
 P = 128
 COEFFS = 16
@@ -31,7 +32,8 @@ QUAD_P = P // QUADS
 QUAD_ROWS = 4
 AHEAD = 2
 H4 = ((1, 1, 1, 1), (1, -1, 1, -1), (1, 1, -1, -1), (1, -1, -1, 1))
-SUMS = 2 * (1 + 2 + 4 + 4)
+LIGHT = 2
+SUMS = 2 * (1 + 2 + 2 + 4 + 4)
 
 FLOPS = 2 * COEFFS * BLOCKS * CHANNELS * N_OUT
 
@@ -123,6 +125,7 @@ def tile_iwht2layer_pa_e_kernel(tc, trans, weight_words, weight_scales, bias, ou
         scales_of = {}
 
         def prepare(phase):
+            heavy = phase >= LIGHT
             for u1 in range(2):
                 x_words = x_of[phase][:, u1, :].bitcast(F32)
                 x_t = psum_x.tile([P, PASSES, 2, P], F32)
@@ -136,7 +139,7 @@ def tile_iwht2layer_pa_e_kernel(tc, trans, weight_words, weight_scales, bias, ou
 
                 grouped_of = []
                 for v0 in range(2):
-                    copies = 1 + v0
+                    copies = 1 + v0 if heavy else 1
                     grouped = stage.tile(
                         [P, copies * PASSES * K_PASS], BF16, align_bytes=64, name="grouped%d" % v0
                     )
@@ -158,13 +161,14 @@ def tile_iwht2layer_pa_e_kernel(tc, trans, weight_words, weight_scales, bias, ou
                         )
                         nc.scalar.mul(out=by_i1[:, :, 1, :], in_=by_i1[:, :, 0, :], mul=-1.0)
 
-                nc.vector.tensor_scalar_mul(
-                    out=grouped_of[1][:, PASSES * K_PASS :],
-                    in0=grouped_of[1][:, 0 : PASSES * K_PASS],
-                    scalar1=-1.0,
-                )
+                if heavy:
+                    nc.vector.tensor_scalar_mul(
+                        out=grouped_of[1][:, PASSES * K_PASS :],
+                        in0=grouped_of[1][:, 0 : PASSES * K_PASS],
+                        scalar1=-1.0,
+                    )
                 for v0 in range(2):
-                    copies = 1 + v0
+                    copies = 1 + v0 if heavy else 1
                     t = coefficient(phase, u1, v0)
                     codes = operands.tile(
                         [P, copies * PASSES * P], U32, align_bytes=64, name="codes%d" % v0
@@ -183,11 +187,12 @@ def tile_iwht2layer_pa_e_kernel(tc, trans, weight_words, weight_scales, bias, ou
             for j0 in range(2):
                 z = psum_z.tile([P, N_OUT], F32, name="z")
                 z_of.append(z)
+            heavy = phase >= LIGHT
             for u1 in range(2):
                 for v0 in range(2):
                     t = coefficient(phase, u1, v0)
-                    for j0 in range(2):
-                        copy = j0 * v0
+                    for j0 in (0, 1) if heavy else (v0,):
+                        copy = j0 * v0 if heavy else 0
                         for g in range(PASSES):
                             cols = slice((copy * PASSES + g) * P, (copy * PASSES + g + 1) * P)
                             k = QUAD_ROWS * (PASSES * v0 + g)
@@ -197,12 +202,24 @@ def tile_iwht2layer_pa_e_kernel(tc, trans, weight_words, weight_scales, bias, ou
                                 lhsT_scale=scales_of[t][:, cols],
                                 rhs=w_of[t][:, g, :].bitcast(FP8X4),
                                 rhs_scale=w_planes[k:P, pair_index(phase, u1), :],
-                                start=(u1 == 0 and v0 == 0 and g == 0),
-                                stop=(u1 == 1 and v0 == 1 and g == PASSES - 1),
+                                start=(u1 == 0 and (v0 == 0 or not heavy) and g == 0),
+                                stop=(u1 == 1 and (v0 == 1 or not heavy) and g == PASSES - 1),
                             )
             return z_of
 
         sum_of = [{(): bias_all}, {(): bias_all}]
+
+        def from_v0_to_j0():
+            both = [{}, {}]
+            for signs in sum_of[0]:
+                for j0 in range(2):
+                    acc = sums.tile([P, N_OUT], F32, name="acc")
+                    nc.vector.tensor_tensor(
+                        out=acc[:], in0=sum_of[0][signs][:], in1=sum_of[1][signs][:], op=(ADD, SUBTRACT)[j0]
+                    )
+                    both[j0][signs] = acc
+            sum_of[0] = both[0]
+            sum_of[1] = both[1]
 
         def combine(phase, z_of):
             for j0 in range(2):
@@ -212,14 +229,17 @@ def tile_iwht2layer_pa_e_kernel(tc, trans, weight_words, weight_scales, bias, ou
                     if signs in longer:
                         continue
                     acc = sums.tile([P, N_OUT], F32, name="acc")
-                    nc.vector.scalar_tensor_tensor(
-                        out=acc[:],
-                        in0=z_of[j0][:],
-                        scalar=signs[-1] / COEFFS,
-                        in1=sum_of[j0][signs[:-1]][:],
-                        op0=MULT,
-                        op1=ADD,
-                    )
+                    if phase == 0 and j0 == 1 and LIGHT > 0:
+                        nc.scalar.mul(out=acc[:], in_=z_of[j0][:], mul=signs[-1] / COEFFS)
+                    else:
+                        nc.vector.scalar_tensor_tensor(
+                            out=acc[:],
+                            in0=z_of[j0][:],
+                            scalar=signs[-1] / COEFFS,
+                            in1=sum_of[j0][signs[:-1]][:],
+                            op0=MULT,
+                            op1=ADD,
+                        )
                     longer[signs] = acc
                     if phase == PHASES - 1:
                         i0, j1 = divmod(o, 2)
@@ -231,5 +251,7 @@ def tile_iwht2layer_pa_e_kernel(tc, trans, weight_words, weight_scales, bias, ou
         spread_bias()
         for phase in range(PHASES):
             combine(phase, multiply(phase))
+            if phase == LIGHT - 1:
+                from_v0_to_j0()
             if phase + AHEAD < PHASES:
                 prepare(phase + AHEAD)

@@ -33,7 +33,8 @@ QUAD_ROWS = 4
 AHEAD = 2
 H4 = ((1, 1, 1, 1), (1, -1, 1, -1), (1, 1, -1, -1), (1, -1, -1, 1))
 LIGHT = 2
-SUMS = 2 * (1 + 2 + 2 + 4 + 4)
+LAST_PARTS = 2
+SUMS = 2 * (1 + 2 + 2 + 4 + 4 * LAST_PARTS)
 
 FLOPS = 2 * COEFFS * BLOCKS * CHANNELS * N_OUT
 
@@ -44,6 +45,11 @@ def pair_index(phase, u1):
 
 def coefficient(phase, u1, v0):
     return 2 * pair_index(phase, u1) + v0
+
+
+def parts_of(phase):
+    count = LAST_PARTS if phase == PHASES - 1 else 1
+    return [(part * (N_OUT // count), N_OUT // count) for part in range(count)]
 
 
 def tile_iwht2layer_pa_e_kernel(tc, trans, weight_words, weight_scales, bias, out):
@@ -77,15 +83,18 @@ def tile_iwht2layer_pa_e_kernel(tc, trans, weight_words, weight_scales, bias, ou
             x_of[phase] = x_sb
 
         def load_w(phase):
-            for u1 in range(2):
-                for v0 in range(2):
-                    t = coefficient(phase, u1, v0)
-                    w_sb = resident.tile([P, PASSES, N_OUT], U32, name="w%d" % t, align_bytes=64)
-                    nc.sync.dma_start(
-                        out=w_sb[:].bitcast(I32),
-                        in_=w_view[:, PASSES * t : PASSES * (t + 1), :].bitcast(I32),
-                    )
-                    w_of[t] = w_sb
+            for first, width in parts_of(phase):
+                for u1 in range(2):
+                    for v0 in range(2):
+                        t = coefficient(phase, u1, v0)
+                        w_sb = resident.tile([P, PASSES, width], U32, name="w%d_%d" % (t, first), align_bytes=64)
+                        nc.sync.dma_start(
+                            out=w_sb[:].bitcast(I32),
+                            in_=w_view[
+                                :, PASSES * t : PASSES * (t + 1), PACK * first : PACK * (first + width)
+                            ].bitcast(I32),
+                        )
+                        w_of[(t, first)] = w_sb
 
         w_planes = const.tile([P, PAIRS, N_OUT], U8, align_bytes=64)
         nc.vector.memset(w_planes[:].bitcast(I32), 0)
@@ -182,10 +191,10 @@ def tile_iwht2layer_pa_e_kernel(tc, trans, weight_words, weight_scales, bias, ou
                     codes_of[t] = codes
                     scales_of[t] = x_scales
 
-        def multiply(phase):
+        def multiply(phase, first, width):
             z_of = []
             for j0 in range(2):
-                z = psum_z.tile([P, N_OUT], F32, name="z")
+                z = psum_z.tile([P, width], F32, name="z")
                 z_of.append(z)
             heavy = phase >= LIGHT
             for u1 in range(2):
@@ -200,8 +209,8 @@ def tile_iwht2layer_pa_e_kernel(tc, trans, weight_words, weight_scales, bias, ou
                                 out=z_of[j0][:],
                                 lhsT=codes_of[t][:, cols].bitcast(FP8X4),
                                 lhsT_scale=scales_of[t][:, cols],
-                                rhs=w_of[t][:, g, :].bitcast(FP8X4),
-                                rhs_scale=w_planes[k:P, pair_index(phase, u1), :],
+                                rhs=w_of[(t, first)][:, g, :].bitcast(FP8X4),
+                                rhs_scale=w_planes[k:P, pair_index(phase, u1), first : first + width],
                                 start=(u1 == 0 and (v0 == 0 or not heavy) and g == 0),
                                 stop=(u1 == 1 and (v0 == 1 or not heavy) and g == PASSES - 1),
                             )
@@ -221,14 +230,14 @@ def tile_iwht2layer_pa_e_kernel(tc, trans, weight_words, weight_scales, bias, ou
             sum_of[0] = both[0]
             sum_of[1] = both[1]
 
-        def combine(phase, z_of):
+        def combine(phase, first, width, z_of):
             for j0 in range(2):
                 longer = {}
                 for o in range(len(H4)):
                     signs = H4[o][: phase + 1]
                     if signs in longer:
                         continue
-                    acc = sums.tile([P, N_OUT], F32, name="acc")
+                    acc = sums.tile([P, width], F32, name="acc")
                     if phase == 0 and j0 == 1 and LIGHT > 0:
                         nc.scalar.mul(out=acc[:], in_=z_of[j0][:], mul=signs[-1] / COEFFS)
                     else:
@@ -236,21 +245,23 @@ def tile_iwht2layer_pa_e_kernel(tc, trans, weight_words, weight_scales, bias, ou
                             out=acc[:],
                             in0=z_of[j0][:],
                             scalar=signs[-1] / COEFFS,
-                            in1=sum_of[j0][signs[:-1]][:],
+                            in1=sum_of[j0][signs[:-1]][:, first : first + width],
                             op0=MULT,
                             op1=ADD,
                         )
                     longer[signs] = acc
                     if phase == PHASES - 1:
                         i0, j1 = divmod(o, 2)
-                        nc.sync.dma_start(out=out_view[i0, j1, j0], in_=acc[:])
-                sum_of[j0] = longer
+                        nc.sync.dma_start(out=out_view[i0, j1, j0][:, :, first : first + width], in_=acc[:])
+                if phase < PHASES - 1:
+                    sum_of[j0] = longer
 
         for phase in range(AHEAD):
             prepare(phase)
         spread_bias()
         for phase in range(PHASES):
-            combine(phase, multiply(phase))
+            for first, width in parts_of(phase):
+                combine(phase, first, width, multiply(phase, first, width))
             if phase == LIGHT - 1:
                 from_v0_to_j0()
             if phase + AHEAD < PHASES:

@@ -30,9 +30,12 @@ PLANES = 2 * PASSES
 QUADS = 4
 QUAD_P = P // QUADS
 QUAD_ROWS = 4
-AHEAD = 2
+AHEAD = 3
+X_BANKS = 2
+Z_BANKS = 6
 H4 = ((1, 1, 1, 1), (1, -1, 1, -1), (1, 1, -1, -1), (1, -1, -1, 1))
 LIGHT = 2
+HELPED = (2, 3)
 LAST_PARTS = 2
 SUMS = 2 * (1 + 2 + 2 + 4 + 4 * LAST_PARTS)
 
@@ -60,8 +63,9 @@ def tile_iwht2layer_pa_e_kernel(tc, trans, weight_words, weight_scales, bias, ou
         stage = ctx.enter_context(tc.tile_pool(name="stage", bufs=2 * AHEAD))
         operands = ctx.enter_context(tc.tile_pool(name="operands", bufs=2 * (AHEAD + 1)))
         sums = ctx.enter_context(tc.tile_pool(name="sums", bufs=SUMS))
-        psum_x = ctx.enter_context(tc.psum_pool(name="psum_x", bufs=2 * AHEAD))
-        psum_z = ctx.enter_context(tc.psum_pool(name="psum_z", bufs=2 * 2))
+        scaled_pool = ctx.enter_context(tc.tile_pool(name="scaled", bufs=2))
+        psum_x = ctx.enter_context(tc.psum_pool(name="psum_x", bufs=X_BANKS))
+        psum_z = ctx.enter_context(tc.psum_pool(name="psum_z", bufs=Z_BANKS))
 
         x_view = trans.rearrange("t b h w c -> (t b h w) c").rearrange(
             "(u1 phase p) c -> phase p u1 c", u1=2, phase=PHASES, p=P
@@ -111,10 +115,11 @@ def tile_iwht2layer_pa_e_kernel(tc, trans, weight_words, weight_scales, bias, ou
         load_x(0)
         load_scales()
         load_x(1)
-        for phase in range(PHASES):
+        load_w(0)
+        load_x(2)
+        load_x(3)
+        for phase in range(1, PHASES):
             load_w(phase)
-            if phase + AHEAD < PHASES:
-                load_x(phase + AHEAD)
 
         ident = const.tile([P, P], F32)
         make_identity(nc, ident[:])
@@ -231,8 +236,13 @@ def tile_iwht2layer_pa_e_kernel(tc, trans, weight_words, weight_scales, bias, ou
             sum_of[1] = both[1]
 
         def combine(phase, first, width, z_of):
+            late_stores = []
             for j0 in range(2):
                 longer = {}
+                helped = HELPED if phase >= LIGHT and j0 == 1 else ()
+                if helped:
+                    scaled = scaled_pool.tile([P, width], F32, name="scaled")
+                    nc.scalar.mul(out=scaled[:], in_=z_of[j0][:], mul=1.0 / COEFFS)
                 for o in range(len(H4)):
                     signs = H4[o][: phase + 1]
                     if signs in longer:
@@ -240,6 +250,13 @@ def tile_iwht2layer_pa_e_kernel(tc, trans, weight_words, weight_scales, bias, ou
                     acc = sums.tile([P, width], F32, name="acc")
                     if phase == 0 and j0 == 1 and LIGHT > 0:
                         nc.scalar.mul(out=acc[:], in_=z_of[j0][:], mul=signs[-1] / COEFFS)
+                    elif o in helped:
+                        nc.gpsimd.tensor_tensor(
+                            out=acc[:],
+                            in0=sum_of[j0][signs[:-1]][:, first : first + width],
+                            in1=scaled[:],
+                            op=ADD if signs[-1] > 0 else SUBTRACT,
+                        )
                     else:
                         nc.vector.scalar_tensor_tensor(
                             out=acc[:],
@@ -252,9 +269,15 @@ def tile_iwht2layer_pa_e_kernel(tc, trans, weight_words, weight_scales, bias, ou
                     longer[signs] = acc
                     if phase == PHASES - 1:
                         i0, j1 = divmod(o, 2)
-                        nc.sync.dma_start(out=out_view[i0, j1, j0][:, :, first : first + width], in_=acc[:])
+                        where = out_view[i0, j1, j0][:, :, first : first + width]
+                        if o in helped:
+                            late_stores.append((where, acc))
+                        else:
+                            nc.sync.dma_start(out=where, in_=acc[:])
                 if phase < PHASES - 1:
                     sum_of[j0] = longer
+            for where, acc in late_stores:
+                nc.sync.dma_start(out=where, in_=acc[:])
 
         for phase in range(AHEAD):
             prepare(phase)

@@ -26,7 +26,7 @@ PASSES = CHANNELS // K_PASS
 PASS_WORDS = K_PASS // 2
 PHASES = 4
 PAIRS = COEFFS // 2
-PLANES = 2 * PASSES
+PLANE_STEP = 8
 QUADS = 4
 QUAD_P = P // QUADS
 QUAD_ROWS = 4
@@ -71,9 +71,7 @@ def tile_iwht2layer_pa_e_kernel(tc, trans, weight_words, weight_scales, bias, ou
             "(u1 phase p) c -> phase p u1 c", u1=2, phase=PHASES, p=P
         )
         w_view = weight_words.rearrange("g p n e -> p g (n e)")
-        s_view = weight_scales.rearrange(
-            "(pair plane) (quad r) n -> quad r plane pair n", plane=PLANES, r=QUAD_ROWS
-        )
+        s_view = weight_scales.rearrange("(t g) (quad r) n -> g r quad t n", g=PASSES, r=QUAD_ROWS)
         out_view = out.rearrange(
             "b (h i1 i0) (w j1 j0) n -> i0 j1 j0 (b h i1) w n", i1=2, i0=2, j1=2, j0=2
         )
@@ -86,48 +84,49 @@ def tile_iwht2layer_pa_e_kernel(tc, trans, weight_words, weight_scales, bias, ou
             nc.sync.dma_start(out=x_sb[:], in_=x_view[phase])
             x_of[phase] = x_sb
 
+        def load_w_of(t, first, width):
+            w_sb = resident.tile([P, PASSES, width], U32, name="w%d_%d" % (t, first), align_bytes=64)
+            nc.sync.dma_start(
+                out=w_sb[:].bitcast(I32),
+                in_=w_view[:, PASSES * t : PASSES * (t + 1), PACK * first : PACK * (first + width)].bitcast(I32),
+            )
+            w_of[(t, first)] = w_sb
+
         def load_w(phase):
             for first, width in parts_of(phase):
                 for u1 in range(2):
                     for v0 in range(2):
-                        t = coefficient(phase, u1, v0)
-                        w_sb = resident.tile([P, PASSES, width], U32, name="w%d_%d" % (t, first), align_bytes=64)
-                        nc.sync.dma_start(
-                            out=w_sb[:].bitcast(I32),
-                            in_=w_view[
-                                :, PASSES * t : PASSES * (t + 1), PACK * first : PACK * (first + width)
-                            ].bitcast(I32),
-                        )
-                        w_of[(t, first)] = w_sb
+                        load_w_of(coefficient(phase, u1, v0), first, width)
 
-        w_planes = const.tile([P, PAIRS, N_OUT], U8, align_bytes=64)
-        nc.vector.memset(w_planes[:].bitcast(I32), 0)
+        w_planes = const.tile([P, COEFFS, N_OUT], U8, align_bytes=64)
+        nc.vector.memset(w_planes[:, 0 : COEFFS // 2, :].bitcast(I32), 0)
+        nc.gpsimd.memset(w_planes[:, COEFFS // 2 :, :].bitcast(F32), 0.0)
+        bias_row = const.tile([P, N_OUT], BF16)
+        nc.vector.memset(bias_row[:], 0.0)
 
         def load_scales():
-            for quad in range(QUADS):
-                for r in range(QUAD_ROWS):
-                    first = QUAD_P * quad + r
+            for r in range(QUAD_ROWS):
+                for g in range(PASSES):
+                    first = PLANE_STEP * g + r
                     nc.sync.dma_start(
-                        out=w_planes[first : first + QUAD_ROWS * PLANES : QUAD_ROWS, :, :].bitcast(I32),
-                        in_=s_view[quad, r].bitcast(I32),
+                        out=w_planes[first:P:QUAD_P, :, :].bitcast(I32), in_=s_view[g, r].bitcast(I32)
                     )
 
-        load_x(0)
-        load_scales()
-        load_x(1)
-        load_w(0)
-        load_x(2)
-        load_x(3)
-        for phase in range(1, PHASES):
-            load_w(phase)
+        with tc.manual_schedule(engines={mybir.EngineType.SP}):
+            load_x(0)
+            load_scales()
+            nc.sync.dma_start(out=bias_row[0:1, :], in_=bias.rearrange("a b c n -> (a b c) n"))
+            load_x(1)
+            load_w(0)
+            load_x(2)
+            load_x(3)
+            for phase in range(1, PHASES):
+                load_w(phase)
 
         ident = const.tile([P, P], F32)
         make_identity(nc, ident[:])
         ones = const.tile([P, P], BF16)
         nc.vector.memset(ones[:], 1.0)
-        bias_row = const.tile([P, N_OUT], BF16)
-        nc.vector.memset(bias_row[:], 0.0)
-        nc.scalar.dma_start(out=bias_row[0:1, :], in_=bias.rearrange("a b c n -> (a b c) n"))
         bias_all = const.tile([P, N_OUT], F32)
 
         def spread_bias():
@@ -209,13 +208,13 @@ def tile_iwht2layer_pa_e_kernel(tc, trans, weight_words, weight_scales, bias, ou
                         copy = j0 * v0 if heavy else 0
                         for g in range(PASSES):
                             cols = slice((copy * PASSES + g) * P, (copy * PASSES + g + 1) * P)
-                            k = QUAD_ROWS * (PASSES * v0 + g)
+                            k = PLANE_STEP * g
                             nc.tensor.matmul_mx(
                                 out=z_of[j0][:],
                                 lhsT=codes_of[t][:, cols].bitcast(FP8X4),
                                 lhsT_scale=scales_of[t][:, cols],
                                 rhs=w_of[(t, first)][:, g, :].bitcast(FP8X4),
-                                rhs_scale=w_planes[k:P, pair_index(phase, u1), first : first + width],
+                                rhs_scale=w_planes[k:P, t, first : first + width],
                                 start=(u1 == 0 and (v0 == 0 or not heavy) and g == 0),
                                 stop=(u1 == 1 and (v0 == 1 or not heavy) and g == PASSES - 1),
                             )

@@ -30,7 +30,7 @@ PLANE_STEP = 8
 QUADS = 4
 QUAD_P = P // QUADS
 QUAD_ROWS = 4
-AHEAD = 3
+AHEAD = 4
 X_BANKS = 2
 Z_BANKS = 6
 H4 = ((1, 1, 1, 1), (1, -1, 1, -1), (1, 1, -1, -1), (1, -1, -1, 1))
@@ -60,8 +60,8 @@ def tile_iwht2layer_pa_e_kernel(tc, trans, weight_words, weight_scales, bias, ou
     with ExitStack() as ctx:
         const = ctx.enter_context(tc.tile_pool(name="const", bufs=1))
         resident = ctx.enter_context(tc.tile_pool(name="resident", bufs=1))
-        stage = ctx.enter_context(tc.tile_pool(name="stage", bufs=2 * AHEAD))
-        operands = ctx.enter_context(tc.tile_pool(name="operands", bufs=2 * (AHEAD + 1)))
+        stage = ctx.enter_context(tc.tile_pool(name="stage", bufs=4))
+        operands = ctx.enter_context(tc.tile_pool(name="operands", bufs=2 * PHASES))
         sums = ctx.enter_context(tc.tile_pool(name="sums", bufs=SUMS))
         scaled_pool = ctx.enter_context(tc.tile_pool(name="scaled", bufs=2))
         psum_x = ctx.enter_context(tc.psum_pool(name="psum_x", bufs=X_BANKS))
@@ -84,19 +84,24 @@ def tile_iwht2layer_pa_e_kernel(tc, trans, weight_words, weight_scales, bias, ou
             nc.sync.dma_start(out=x_sb[:], in_=x_view[phase])
             x_of[phase] = x_sb
 
-        def load_w_of(t, first, width):
+        def load_w_of(t, first, width, pieces):
             w_sb = resident.tile([P, PASSES, width], U32, name="w%d_%d" % (t, first), align_bytes=64)
-            nc.sync.dma_start(
-                out=w_sb[:].bitcast(I32),
-                in_=w_view[:, PASSES * t : PASSES * (t + 1), PACK * first : PACK * (first + width)].bitcast(I32),
-            )
+            step = PASSES // pieces
+            for g in range(0, PASSES, step):
+                nc.sync.dma_start(
+                    out=w_sb[:, g : g + step, :].bitcast(I32),
+                    in_=w_view[
+                        :, PASSES * t + g : PASSES * t + g + step, PACK * first : PACK * (first + width)
+                    ].bitcast(I32),
+                )
             w_of[(t, first)] = w_sb
 
         def load_w(phase):
             for first, width in parts_of(phase):
                 for u1 in range(2):
                     for v0 in range(2):
-                        load_w_of(coefficient(phase, u1, v0), first, width)
+                        last = phase >= LIGHT and u1 == 1 and v0 == 1
+                        load_w_of(coefficient(phase, u1, v0), first, width, PASSES if last else 1)
 
         w_planes = const.tile([P, COEFFS, N_OUT], U8, align_bytes=64)
         nc.vector.memset(w_planes[:, 0 : COEFFS // 2, :].bitcast(I32), 0)
@@ -116,11 +121,9 @@ def tile_iwht2layer_pa_e_kernel(tc, trans, weight_words, weight_scales, bias, ou
             load_x(0)
             load_scales()
             nc.sync.dma_start(out=bias_row[0:1, :], in_=bias.rearrange("a b c n -> (a b c) n"))
-            load_x(1)
-            load_w(0)
-            load_x(2)
-            load_x(3)
             for phase in range(1, PHASES):
+                load_x(phase)
+            for phase in range(PHASES):
                 load_w(phase)
 
         ident = const.tile([P, P], F32)
@@ -172,7 +175,7 @@ def tile_iwht2layer_pa_e_kernel(tc, trans, weight_words, weight_scales, bias, ou
                         by_i1 = grouped_of[v0][:, 0 : PASSES * K_PASS].rearrange(
                             "p (gm i1 wc) -> p gm i1 wc", i1=2, wc=W * PACK
                         )
-                        nc.scalar.mul(out=by_i1[:, :, 1, :], in_=by_i1[:, :, 0, :], mul=-1.0)
+                        nc.vector.tensor_scalar_mul(out=by_i1[:, :, 1, :], in0=by_i1[:, :, 0, :], scalar1=-1.0)
 
                 if heavy:
                     nc.vector.tensor_scalar_mul(
@@ -204,9 +207,9 @@ def tile_iwht2layer_pa_e_kernel(tc, trans, weight_words, weight_scales, bias, ou
             for u1 in range(2):
                 for v0 in range(2):
                     t = coefficient(phase, u1, v0)
-                    for j0 in (0, 1) if heavy else (v0,):
-                        copy = j0 * v0 if heavy else 0
-                        for g in range(PASSES):
+                    for g in range(PASSES):
+                        for j0 in (0, 1) if heavy else (v0,):
+                            copy = j0 * v0 if heavy else 0
                             cols = slice((copy * PASSES + g) * P, (copy * PASSES + g + 1) * P)
                             k = PLANE_STEP * g
                             nc.tensor.matmul_mx(

@@ -237,15 +237,14 @@ def tile_iwht2layer_pa_e_kernel(tc, trans, weight_words, weight_scales, bias, ou
             sum_of[0] = both[0]
             sum_of[1] = both[1]
 
-        def combine(phase, first, width, z_of):
-            late_stores = []
-            for j0 in range(2):
+        def combine(phase, first, width, z_of, which_j0):
+            for j0 in which_j0:
                 longer = {}
                 helped = HELPED if phase >= LIGHT and j0 == 1 else ()
                 if helped:
                     scaled = scaled_pool.tile([P, width], F32, name="scaled")
                     nc.scalar.mul(out=scaled[:], in_=z_of[j0][:], mul=1.0 / COEFFS)
-                for o in range(len(H4)):
+                for o in helped + tuple([other for other in range(len(H4)) if other not in helped]):
                     signs = H4[o][: phase + 1]
                     if signs in longer:
                         continue
@@ -271,23 +270,22 @@ def tile_iwht2layer_pa_e_kernel(tc, trans, weight_words, weight_scales, bias, ou
                     longer[signs] = acc
                     if phase == PHASES - 1:
                         i0, j1 = divmod(o, 2)
-                        where = out_view[i0, j1, j0][:, :, first : first + width]
-                        if o in helped:
-                            late_stores.append((where, acc))
-                        else:
-                            nc.sync.dma_start(out=where, in_=acc[:])
+                        nc.sync.dma_start(out=out_view[i0, j1, j0][:, :, first : first + width], in_=acc[:])
                 if phase < PHASES - 1:
                     sum_of[j0] = longer
-            for where, acc in late_stores:
-                nc.sync.dma_start(out=where, in_=acc[:])
 
         for phase in range(AHEAD):
             prepare(phase)
         spread_bias()
-        for phase in range(PHASES):
-            for first, width in parts_of(phase):
-                combine(phase, first, width, multiply(phase, first, width))
+        for phase in range(PHASES - 2):
+            combine(phase, 0, N_OUT, multiply(phase, 0, N_OUT), (0, 1))
             if phase == LIGHT - 1:
                 from_v0_to_j0()
-            if phase + AHEAD < PHASES:
-                prepare(phase + AHEAD)
+        before_last = multiply(PHASES - 2, 0, N_OUT)
+        ranges = parts_of(PHASES - 1)
+        first_range = multiply(PHASES - 1, ranges[0][0], ranges[0][1])
+        for j0 in range(2):
+            combine(PHASES - 2, 0, N_OUT, before_last, (j0,))
+            combine(PHASES - 1, ranges[0][0], ranges[0][1], first_range, (j0,))
+        for first, width in ranges[1:]:
+            combine(PHASES - 1, first, width, multiply(PHASES - 1, first, width), (0, 1))

from contextlib import ExitStack

import concourse.mybir as mybir
from concourse.masks import make_identity

F32 = mybir.dt.float32
BF16 = mybir.dt.bfloat16
I32 = mybir.dt.int32
U32 = mybir.dt.uint32
U8 = mybir.dt.uint8
FP8X4 = mybir.dt.float8_e4m3fn_x4
MULT = mybir.AluOpType.mult
ADD = mybir.AluOpType.add
SUBTRACT = mybir.AluOpType.subtract

P = 128
COEFFS = 16
BLOCKS = 64
BH = 16
W = 4
CHANNELS = 1024
N_OUT = 512
PACK = 4
K_PASS = P * PACK
PASSES = CHANNELS // K_PASS
PASS_WORDS = K_PASS // 2
PHASES = 4
PAIRS = COEFFS // 2
PLANE_STEP = 8
QUADS = 4
QUAD_P = P // QUADS
QUAD_ROWS = 4
AHEAD = 4
X_BANKS = 2
Z_BANKS = 6
H4 = ((1, 1, 1, 1), (1, -1, 1, -1), (1, 1, -1, -1), (1, -1, -1, 1))
LIGHT = 2
HELPED = (2, 3)
LAST_PARTS = 2
SUMS = 2 * (1 + 2 + 2 + 4 + 4 * LAST_PARTS)

FLOPS = 2 * COEFFS * BLOCKS * CHANNELS * N_OUT


def pair_index(phase, u1):
    return PHASES * u1 + phase


def coefficient(phase, u1, v0):
    return 2 * pair_index(phase, u1) + v0


def parts_of(phase):
    count = LAST_PARTS if phase == PHASES - 1 else 1
    return [(part * (N_OUT // count), N_OUT // count) for part in range(count)]


def tile_iwht2layer_pa_e_kernel(tc, trans, weight_words, weight_scales, bias, out):
    nc = tc.nc
    with ExitStack() as ctx:
        const = ctx.enter_context(tc.tile_pool(name="const", bufs=1))
        resident = ctx.enter_context(tc.tile_pool(name="resident", bufs=1))
        stage = ctx.enter_context(tc.tile_pool(name="stage", bufs=4))
        operands = ctx.enter_context(tc.tile_pool(name="operands", bufs=2 * PHASES))
        sums = ctx.enter_context(tc.tile_pool(name="sums", bufs=SUMS))
        scaled_pool = ctx.enter_context(tc.tile_pool(name="scaled", bufs=2))
        psum_x = ctx.enter_context(tc.psum_pool(name="psum_x", bufs=X_BANKS))
        psum_z = ctx.enter_context(tc.psum_pool(name="psum_z", bufs=Z_BANKS))

        x_view = trans.rearrange("t b h w c -> (t b h w) c").rearrange(
            "(u1 phase p) c -> phase p u1 c", u1=2, phase=PHASES, p=P
        )
        w_view = weight_words.rearrange("g p n e -> p g (n e)")
        s_view = weight_scales.rearrange("(t g) (quad r) n -> g r quad t n", g=PASSES, r=QUAD_ROWS)
        out_view = out.rearrange(
            "b (h i1 i0) (w j1 j0) n -> i0 j1 j0 (b h i1) w n", i1=2, i0=2, j1=2, j0=2
        )

        x_of = {}
        w_of = {}

        def load_x(phase):
            x_sb = resident.tile([P, 2, CHANNELS], BF16, name="x%d" % phase)
            nc.sync.dma_start(out=x_sb[:], in_=x_view[phase])
            x_of[phase] = x_sb

        def load_w_of(t, first, width, pieces):
            w_sb = resident.tile([P, PASSES, width], U32, name="w%d_%d" % (t, first), align_bytes=64)
            step = PASSES // pieces
            for g in range(0, PASSES, step):
                nc.sync.dma_start(
                    out=w_sb[:, g : g + step, :].bitcast(I32),
                    in_=w_view[
                        :, PASSES * t + g : PASSES * t + g + step, PACK * first : PACK * (first + width)
                    ].bitcast(I32),
                )
            w_of[(t, first)] = w_sb

        def load_w(phase):
            for first, width in parts_of(phase):
                for u1 in range(2):
                    for v0 in range(2):
                        last = phase >= LIGHT and u1 == 1 and v0 == 1
                        load_w_of(coefficient(phase, u1, v0), first, width, PASSES if last else 1)

        w_planes = const.tile([P, COEFFS, N_OUT], U8, align_bytes=64)
        nc.vector.memset(w_planes[:, 0 : COEFFS // 2, :].bitcast(I32), 0)
        nc.gpsimd.memset(w_planes[:, COEFFS // 2 :, :].bitcast(F32), 0.0)
        bias_row = const.tile([P, N_OUT], BF16)
        nc.vector.memset(bias_row[:], 0.0)

        def load_scales():
            for r in range(QUAD_ROWS):
                for g in range(PASSES):
                    first = PLANE_STEP * g + r
                    nc.sync.dma_start(
                        out=w_planes[first:P:QUAD_P, :, :].bitcast(I32), in_=s_view[g, r].bitcast(I32)
                    )

        with tc.manual_schedule(engines={mybir.EngineType.SP}):
            load_x(0)
            load_scales()
            nc.sync.dma_start(out=bias_row[0:1, :], in_=bias.rearrange("a b c n -> (a b c) n"))
            for phase in range(1, PHASES):
                load_x(phase)
            for phase in range(PHASES):
                load_w(phase)

        ident = const.tile([P, P], F32)
        make_identity(nc, ident[:])
        ones = const.tile([P, P], BF16)
        nc.vector.memset(ones[:], 1.0)
        bias_all = const.tile([P, N_OUT], F32)

        def spread_bias():
            bias_ps = psum_z.tile([P, N_OUT], F32, name="z")
            nc.tensor.matmul(out=bias_ps[:], lhsT=ones[:], rhs=bias_row[:], start=True, stop=True)
            nc.scalar.copy(out=bias_all[:], in_=bias_ps[:])

        codes_of = {}
        scales_of = {}

        def prepare(phase):
            heavy = phase >= LIGHT
            for u1 in range(2):
                x_words = x_of[phase][:, u1, :].bitcast(F32)
                x_t = psum_x.tile([P, PASSES, 2, P], F32)
                for g in range(PASSES):
                    for half in range(2):
                        nc.tensor.transpose(
                            x_t[:, g, half, :],
                            x_words[:, PASS_WORDS * g + half : PASS_WORDS * (g + 1) : 2],
                            ident[:],
                        )

                grouped_of = []
                for v0 in range(2):
                    copies = 1 + v0 if heavy else 1
                    grouped = stage.tile(
                        [P, copies * PASSES * K_PASS], BF16, align_bytes=64, name="grouped%d" % v0
                    )
                    grouped_of.append(grouped)
                    as_words = grouped[:].bitcast(F32).rearrange(
                        "p (copy g m i1 w half) -> p copy g m i1 w half",
                        copy=copies, g=PASSES, m=BH, i1=2, w=W, half=2,
                    )
                    rows = x_t[:, :, :, BLOCKS * v0 : BLOCKS * (v0 + 1)].rearrange(
                        "p g half (m w) -> p g m w half", w=W
                    )
                    nc.scalar.copy(out=as_words[:, 0, :, :, 0, :, :], in_=rows)
                    if u1 == 0:
                        nc.scalar.copy(out=as_words[:, 0, :, :, 1, :, :], in_=rows)
                if u1 == 1:
                    for v0 in range(2):
                        by_i1 = grouped_of[v0][:, 0 : PASSES * K_PASS].rearrange(
                            "p (gm i1 wc) -> p gm i1 wc", i1=2, wc=W * PACK
                        )
                        nc.vector.tensor_scalar_mul(out=by_i1[:, :, 1, :], in0=by_i1[:, :, 0, :], scalar1=-1.0)

                if heavy:
                    nc.vector.tensor_scalar_mul(
                        out=grouped_of[1][:, PASSES * K_PASS :],
                        in0=grouped_of[1][:, 0 : PASSES * K_PASS],
                        scalar1=-1.0,
                    )
                for v0 in range(2):
                    copies = 1 + v0 if heavy else 1
                    t = coefficient(phase, u1, v0)
                    codes = operands.tile(
                        [P, copies * PASSES * P], U32, align_bytes=64, name="codes%d" % v0
                    )
                    x_scales = operands.tile(
                        [P, copies * PASSES * P], U8, align_bytes=64, name="x_scales%d" % v0
                    )
                    nc.vector.quantize_mx(
                        out=codes[:].bitcast(FP8X4), scales=x_scales[:], in_=grouped_of[v0][:]
                    )
                    codes_of[t] = codes
                    scales_of[t] = x_scales

        def multiply(phase, first, width):
            z_of = []
            for j0 in range(2):
                z = psum_z.tile([P, width], F32, name="z")
                z_of.append(z)
            heavy = phase >= LIGHT
            for u1 in range(2):
                for v0 in range(2):
                    t = coefficient(phase, u1, v0)
                    for g in range(PASSES):
                        for j0 in (0, 1) if heavy else (v0,):
                            copy = j0 * v0 if heavy else 0
                            cols = slice((copy * PASSES + g) * P, (copy * PASSES + g + 1) * P)
                            k = PLANE_STEP * g
                            nc.tensor.matmul_mx(
                                out=z_of[j0][:],
                                lhsT=codes_of[t][:, cols].bitcast(FP8X4),
                                lhsT_scale=scales_of[t][:, cols],
                                rhs=w_of[(t, first)][:, g, :].bitcast(FP8X4),
                                rhs_scale=w_planes[k:P, t, first : first + width],
                                start=(u1 == 0 and (v0 == 0 or not heavy) and g == 0),
                                stop=(u1 == 1 and (v0 == 1 or not heavy) and g == PASSES - 1),
                            )
            return z_of

        sum_of = [{(): bias_all}, {(): bias_all}]

        def from_v0_to_j0():
            both = [{}, {}]
            for signs in sum_of[0]:
                for j0 in range(2):
                    acc = sums.tile([P, N_OUT], F32, name="acc")
                    nc.vector.tensor_tensor(
                        out=acc[:], in0=sum_of[0][signs][:], in1=sum_of[1][signs][:], op=(ADD, SUBTRACT)[j0]
                    )
                    both[j0][signs] = acc
            sum_of[0] = both[0]
            sum_of[1] = both[1]

        def combine(phase, first, width, z_of, which_j0):
            for j0 in which_j0:
                longer = {}
                helped = HELPED if phase >= LIGHT and j0 == 1 else ()
                if helped:
                    scaled = scaled_pool.tile([P, width], F32, name="scaled")
                    nc.scalar.mul(out=scaled[:], in_=z_of[j0][:], mul=1.0 / COEFFS)
                for o in helped + tuple([other for other in range(len(H4)) if other not in helped]):
                    signs = H4[o][: phase + 1]
                    if signs in longer:
                        continue
                    acc = sums.tile([P, width], F32, name="acc")
                    if phase == 0 and j0 == 1 and LIGHT > 0:
                        nc.scalar.mul(out=acc[:], in_=z_of[j0][:], mul=signs[-1] / COEFFS)
                    elif o in helped:
                        nc.gpsimd.tensor_tensor(
                            out=acc[:],
                            in0=sum_of[j0][signs[:-1]][:, first : first + width],
                            in1=scaled[:],
                            op=ADD if signs[-1] > 0 else SUBTRACT,
                        )
                    else:
                        nc.vector.scalar_tensor_tensor(
                            out=acc[:],
                            in0=z_of[j0][:],
                            scalar=signs[-1] / COEFFS,
                            in1=sum_of[j0][signs[:-1]][:, first : first + width],
                            op0=MULT,
                            op1=ADD,
                        )
                    longer[signs] = acc
                    if phase == PHASES - 1:
                        i0, j1 = divmod(o, 2)
                        nc.sync.dma_start(out=out_view[i0, j1, j0][:, :, first : first + width], in_=acc[:])
                if phase < PHASES - 1:
                    sum_of[j0] = longer

        for phase in range(AHEAD):
            prepare(phase)
        spread_bias()
        for phase in range(PHASES - 2):
            combine(phase, 0, N_OUT, multiply(phase, 0, N_OUT), (0, 1))
            if phase == LIGHT - 1:
                from_v0_to_j0()
        before_last = multiply(PHASES - 2, 0, N_OUT)
        ranges = parts_of(PHASES - 1)
        first_range = multiply(PHASES - 1, ranges[0][0], ranges[0][1])
        for j0 in range(2):
            combine(PHASES - 2, 0, N_OUT, before_last, (j0,))
            combine(PHASES - 1, ranges[0][0], ranges[0][1], first_range, (j0,))
        for first, width in ranges[1:]:
            combine(PHASES - 1, first, width, multiply(PHASES - 1, first, width), (0, 1))
